import numpy as np
import ml_dtypes


def mxq(x, axis, fmt="e4m3"):
    dtype, down = {"e4m3": (ml_dtypes.float8_e4m3fn, 7), "e5m2": (ml_dtypes.float8_e5m2, 14)}[fmt]
    v = np.moveaxis(np.asarray(x, np.float32).astype(ml_dtypes.bfloat16).astype(np.float64), axis, -1)
    blocks = v.reshape(v.shape[:-1] + (-1, 32))
    amax = np.abs(blocks).max(-1, keepdims=True)
    byte = np.maximum(np.where(amax > 0, np.frexp(amax)[1] - 1 + 127, 0) - down, 1)
    scale = np.exp2(byte - 127.0)
    codes = (blocks / scale).astype(np.float32).astype(dtype).astype(np.float64)
    return np.moveaxis((codes * scale).reshape(v.shape), -1, axis)


WIDE = False


def mx_kscale(k):
    if not WIDE:
        return np.ones(k)
    levels = np.array([10, -10, 5, -5, 0])
    a = np.random.permutation(np.resize(levels, k // 512 * 4)).reshape(k // 512, 4)
    idx = np.arange(k)
    return np.exp2(a[idx // 512, idx % 128 // 32])


BF16 = ml_dtypes.bfloat16


def bf(x):
    return np.asarray(x, np.float32).astype(BF16)


def f64(x):
    return np.asarray(x).astype(np.float64)


E2M1 = np.array([0.0, 0.5, 1.0, 1.5, 2.0, 3.0, 4.0, 6.0, -0.0, -0.5, -1.0, -1.5, -2.0, -3.0, -4.0, -6.0])


def pack_weight(w, fmt):
    k, n = w.shape
    w = f64(bf(w)).reshape(k // 32, 32, n)
    amax = np.abs(w).max(1)
    if fmt == "e4m3":
        byte = np.frexp(amax)[1] - 1 + 127 - 7
    else:
        mant, ex = np.frexp(amax / 6.0)
        byte = np.where(mant > 0.5, ex, ex - 1) + 127
    byte = np.clip(np.where(amax > 0, byte, 1), 1, 254)
    scaled = (w * np.exp2(127.0 - byte)[:, None, :]).reshape(k, n).astype(np.float32)
    by_word = np.ascontiguousarray(scaled.reshape(k // 512, 128, 4, n).transpose(0, 1, 3, 2))
    if fmt == "e4m3":
        words = by_word.astype(ml_dtypes.float8_e4m3fn).view(np.uint8)
    else:
        c = by_word.astype(ml_dtypes.float4_e2m1fn).view(np.uint8) & 0xF
        words = c[..., 0::2] | (c[..., 1::2] << 4)
    return np.ascontiguousarray(words), np.ascontiguousarray(byte.astype(np.uint8).reshape(k // 512, 16, n))


def unpack_weight(words, scales, fmt):
    g, p, n, _ = words.shape
    if fmt == "e4m3":
        vals = np.ascontiguousarray(words).view(ml_dtypes.float8_e4m3fn).astype(np.float64)
    else:
        nib = np.empty((g, p, n, 4), np.uint8)
        nib[..., 0::2] = words & 0xF
        nib[..., 1::2] = words >> 4
        vals = E2M1[nib]
    vals = vals * np.repeat(np.exp2(scales.astype(np.float64) - 127.0), 8, axis=1)[..., None]
    return vals.transpose(0, 1, 3, 2).reshape(g * 512, n)


B, H = 1024, 1024
FMT = "e4m3"


def sigmoid(v):
    return 1.0 / (1.0 + np.exp(-v))


def setup_inputs():
    s = mx_kscale(H)
    w = lambda: pack_weight(np.ascontiguousarray((np.random.standard_normal((H, H)) * 0.7 / np.sqrt(H) / s[None, :]).T), FMT)
    b = lambda: bf(np.random.standard_normal(H) * 0.5)
    inputs = bf(np.random.standard_normal((B, H)) * s)
    short_term_memory = bf(np.random.standard_normal((B, H)) * s)
    Wf_words, Wf_scales = w()
    b_f = b()
    Wi_words, Wi_scales = w()
    b_i = b()
    Wg_words, Wg_scales = w()
    b_g = b()
    Wo_words, Wo_scales = w()
    b_o = b()
    return {"inputs": inputs,
            "short_term_memory": short_term_memory,
            "Wf_words": Wf_words, "Wf_scales": Wf_scales, "b_f": b_f,
            "Wi_words": Wi_words, "Wi_scales": Wi_scales, "b_i": b_i,
            "Wg_words": Wg_words, "Wg_scales": Wg_scales, "b_g": b_g,
            "Wo_words": Wo_words, "Wo_scales": Wo_scales, "b_o": b_o}


def reference(inputs, short_term_memory, Wf_words, Wf_scales, b_f, Wi_words, Wi_scales, b_i, Wg_words, Wg_scales, b_g, Wo_words, Wo_scales, b_o):
    z = f64(inputs) + f64(short_term_memory)
    zq = mxq(z, 1, "e4m3")
    c = sigmoid((zq @ unpack_weight(Wf_words, Wf_scales, FMT)) + f64(b_f))
    c = c + sigmoid((zq @ unpack_weight(Wi_words, Wi_scales, FMT)) + f64(b_i)) * np.tanh((zq @ unpack_weight(Wg_words, Wg_scales, FMT)) + f64(b_g))
    h = np.tanh(c) * sigmoid((zq @ unpack_weight(Wo_words, Wo_scales, FMT)) + f64(b_o))
    return np.stack((c, h))

@@ -1,0 +1,223 @@
+from contextlib import ExitStack
+
+import concourse.mybir as mybir
+from concourse.masks import make_identity
+
+F32 = mybir.dt.float32
+BF16 = mybir.dt.bfloat16
+I32 = mybir.dt.int32
+U32 = mybir.dt.uint32
+U8 = mybir.dt.uint8
+FP8X4 = mybir.dt.float8_e4m3fn_x4
+ACT = mybir.ActivationFunctionType
+ALU = mybir.AluOpType
+
+P = 128
+PACK = 4
+K_PASS = P * PACK
+B = 1024
+H = 1024
+K_GROUPS = H // K_PASS
+N_TILES = H // P
+B_TILES = B // P
+B_CHUNK = 512
+CHUNKS = B // B_CHUNK
+TILES_PER_CHUNK = B_CHUNK // P
+PLANE_ROWS = 4
+W_PIECES = 4
+W_PIECE = H // W_PIECES
+STEPS_PER_STORE = 2
+STORE_COLS = STEPS_PER_STORE * P
+Z_PREP_FIRST_STEP = 2
+
+GATES = ("i", "g", "f", "o")
+GATE_FUNC = {"i": ACT.Sigmoid, "g": ACT.Tanh, "f": ACT.Sigmoid, "o": ACT.Sigmoid}
+
+FLOPS = 2 * B * H * 4 * H
+
+
+def tile_lstmcell_pa_kernel(
+    tc,
+    inputs,
+    short_term_memory,
+    Wf_words,
+    Wf_scales,
+    b_f,
+    Wi_words,
+    Wi_scales,
+    b_i,
+    Wg_words,
+    Wg_scales,
+    b_g,
+    Wo_words,
+    Wo_scales,
+    b_o,
+    out,
+):
+    nc = tc.nc
+    words_in = {"i": Wi_words, "g": Wg_words, "f": Wf_words, "o": Wo_words}
+    scales_in = {"i": Wi_scales, "g": Wg_scales, "f": Wf_scales, "o": Wo_scales}
+    bias_in = {"i": b_i, "g": b_g, "f": b_f, "o": b_o}
+    out_view = out.rearrange("o (c t p) n -> o c p t n", t=TILES_PER_CHUNK, p=P)
+
+    with ExitStack() as ctx:
+        keep = ctx.enter_context(tc.tile_pool(name="keep", bufs=1))
+        rows = ctx.enter_context(tc.tile_pool(name="rows", bufs=B_TILES))
+        prep = ctx.enter_context(tc.tile_pool(name="prep", bufs=2))
+        work = ctx.enter_context(tc.tile_pool(name="work", bufs=3))
+        stage = ctx.enter_context(tc.tile_pool(name="stage", bufs=3))
+        gate_banks = ctx.enter_context(tc.psum_pool(name="gate_banks", bufs=4))
+        turn_banks = ctx.enter_context(tc.psum_pool(name="turn_banks", bufs=4))
+
+        ident = keep.tile([P, P], F32)
+        make_identity(nc, ident[:])
+
+        w_planes = keep.tile([P, K_GROUPS, H], U8, align_bytes=64)
+        nc.vector.memset(w_planes[:].bitcast(I32), 0)
+        bias_rows = keep.tile([P, P], BF16)
+        nc.vector.memset(bias_rows[:], 0.0)
+
+        w_codes = {}
+        for gate in GATES:
+            w_codes[gate] = keep.tile([P, K_GROUPS, H], U32, align_bytes=64, name="w_codes_" + gate)
+        z_codes = []
+        z_planes = []
+        for c in range(CHUNKS):
+            z_codes.append(keep.tile([P, K_GROUPS, B_CHUNK], U32, align_bytes=64, name="z_codes%d" % c))
+            z_planes.append(keep.tile([P, K_GROUPS, B_CHUNK], U8, align_bytes=64, name="z_planes%d" % c))
+
+        x_rows = []
+        h_rows = []
+
+        def load_rows(bt):
+            b_rows = slice(bt * P, (bt + 1) * P)
+            x_rows.append(rows.tile([P, H], BF16, name="x_rows"))
+            nc.sync.dma_start(out=x_rows[bt][:], in_=inputs[b_rows, :])
+            h_rows.append(rows.tile([P, H], BF16, name="h_rows"))
+            nc.sync.dma_start(out=h_rows[bt][:], in_=short_term_memory[b_rows, :])
+
+        def load_scales():
+            for q, gate in enumerate(GATES):
+                by_row = scales_in[gate].rearrange("g (Q r) n -> r Q g n", r=PLANE_ROWS)
+                for r in range(PLANE_ROWS):
+                    nc.sync.dma_start(
+                        out=w_planes[PLANE_ROWS * q + r : P : 32, :, :].bitcast(I32),
+                        in_=by_row[r].bitcast(I32),
+                    )
+
+        def load_words(piece):
+            for gate in GATES:
+                by_partition = words_in[gate].rearrange("g p n t -> p g (n t)")
+                nc.sync.dma_start(
+                    out=w_codes[gate][:, :, piece * W_PIECE : (piece + 1) * W_PIECE].bitcast(I32),
+                    in_=by_partition[:, :, piece * W_PIECE * PACK : (piece + 1) * W_PIECE * PACK].bitcast(I32),
+                )
+
+        for q, gate in enumerate(GATES):
+            nc.scalar.dma_start(
+                out=bias_rows[N_TILES * q : N_TILES * (q + 1), :],
+                in_=bias_in[gate].rearrange("(j n) -> j n", n=P),
+            )
+        for bt in range(TILES_PER_CHUNK):
+            load_rows(bt)
+        load_scales()
+        load_words(0)
+        load_words(1)
+        for bt in range(TILES_PER_CHUNK, B_TILES):
+            load_rows(bt)
+        load_words(2)
+        load_words(3)
+
+        bias_f32 = keep.tile([P, P], F32)
+        nc.vector.tensor_copy(out=bias_f32[:], in_=bias_rows[:])
+        bias_bank = turn_banks.tile([P, P], F32, tag="turn")
+        nc.tensor.transpose(bias_bank[:], bias_f32[:], ident[:])
+        bias_cols = keep.tile([P, P], F32)
+        nc.vector.tensor_copy(out=bias_cols[:], in_=bias_bank[:])
+
+        def prepare_z(bt):
+            c = bt // TILES_PER_CHUNK
+            b_cols = slice((bt % TILES_PER_CHUNK) * P, (bt % TILES_PER_CHUNK + 1) * P)
+            z_rows = prep.tile([P, H], BF16)
+            nc.vector.tensor_tensor(out=z_rows[:], in0=x_rows[bt][:], in1=h_rows[bt][:], op=ALU.add)
+            z_words = z_rows[:].bitcast(F32)
+            turned = turn_banks.tile([P, K_GROUPS, 2, P], F32, tag="turn")
+            for g in range(K_GROUPS):
+                for u in range(2):
+                    nc.tensor.transpose(
+                        turned[:, g, u, :],
+                        z_words[:, (K_PASS // 2) * g + u : (K_PASS // 2) * (g + 1) : 2],
+                        ident[:],
+                    )
+            grouped = prep.tile([P, K_GROUPS, P, PACK], BF16, align_bytes=64)
+            nc.vector.tensor_copy(out=grouped[:].bitcast(F32), in_=turned[:].rearrange("p g u b -> p g b u"))
+            for g in range(K_GROUPS):
+                nc.vector.quantize_mx(
+                    out=z_codes[c][:, g, b_cols].bitcast(FP8X4),
+                    scales=z_planes[c][:, g, b_cols],
+                    in_=grouped[:, g, :, :].rearrange("p b t -> p (b t)"),
+                )
+
+        def gates_of(c, j):
+            n_cols = slice(j * P, (j + 1) * P)
+            acts = {}
+            for q, gate in enumerate(GATES):
+                bank = gate_banks.tile([P, B_CHUNK], F32, tag="gate")
+                for g in range(K_GROUPS):
+                    nc.tensor.matmul_mx(
+                        out=bank[:],
+                        lhsT=w_codes[gate][:, g, n_cols].bitcast(FP8X4),
+                        lhsT_scale=w_planes[PLANE_ROWS * q : P, g, n_cols],
+                        rhs=z_codes[c][:, g, :].bitcast(FP8X4),
+                        rhs_scale=z_planes[c][:, g, :],
+                        start=(g == 0),
+                        stop=(g == K_GROUPS - 1),
+                    )
+                acts[gate] = work.tile([P, B_CHUNK], F32, name="act_" + gate)
+                nc.scalar.activation(
+                    out=acts[gate][:],
+                    in_=bank[:],
+                    func=GATE_FUNC[gate],
+                    bias=bias_cols[:, N_TILES * q + j : N_TILES * q + j + 1],
+                    scale=1.0,
+                )
+            cell_t = work.tile([P, B_CHUNK], F32)
+            nc.vector.tensor_tensor(out=cell_t[:], in0=acts["i"][:], in1=acts["g"][:], op=ALU.mult)
+            nc.vector.tensor_tensor(out=cell_t[:], in0=cell_t[:], in1=acts["f"][:], op=ALU.add)
+            return cell_t, acts["o"]
+
+        staged = {}
+
+        def finish(c, j, cell_t, gate_o_t):
+            if j % STEPS_PER_STORE == 0:
+                staged["c"] = stage.tile([P, TILES_PER_CHUNK, STORE_COLS], F32, name="c_stage")
+                staged["h"] = stage.tile([P, TILES_PER_CHUNK, STORE_COLS], F32, name="h_stage")
+            cols = slice((j % STEPS_PER_STORE) * P, (j % STEPS_PER_STORE + 1) * P)
+            c_bank = turn_banks.tile([P, TILES_PER_CHUNK, P], F32, tag="turn")
+            o_bank = turn_banks.tile([P, TILES_PER_CHUNK, P], F32, tag="turn")
+            for t in range(TILES_PER_CHUNK):
+                nc.tensor.transpose(c_bank[:, t, :], cell_t[:, t * P : (t + 1) * P], ident[:])
+            for t in range(TILES_PER_CHUNK):
+                nc.tensor.transpose(o_bank[:, t, :], gate_o_t[:, t * P : (t + 1) * P], ident[:])
+            nc.vector.tensor_copy(out=staged["c"][:, :, cols], in_=c_bank[:])
+            tanh_c = work.tile([P, TILES_PER_CHUNK, P], F32)
+            nc.scalar.activation(out=tanh_c[:], in_=staged["c"][:, :, cols], func=ACT.Tanh)
+            nc.vector.tensor_tensor(out=staged["h"][:, :, cols], in0=o_bank[:], in1=tanh_c[:], op=ALU.mult)
+            if j % STEPS_PER_STORE == STEPS_PER_STORE - 1:
+                n_cols = slice((j + 1) * P - STORE_COLS, (j + 1) * P)
+                nc.sync.dma_start(out=out_view[0, c, :, :, n_cols], in_=staged["c"][:])
+                nc.sync.dma_start(out=out_view[1, c, :, :, n_cols], in_=staged["h"][:])
+
+        for bt in range(TILES_PER_CHUNK):
+            prepare_z(bt)
+        waiting = []
+        for c in range(CHUNKS):
+            for j in range(N_TILES):
+                cell_t, gate_o_t = gates_of(c, j)
+                ahead = j - Z_PREP_FIRST_STEP
+                if c + 1 < CHUNKS and 0 <= ahead < TILES_PER_CHUNK:
+                    prepare_z((c + 1) * TILES_PER_CHUNK + ahead)
+                if waiting:
+                    finish(*waiting.pop())
+                waiting.append((c, j, cell_t, gate_o_t))
+        finish(*waiting.pop())

@@ -63,11 +63,12 @@ def tile_lstmcell_pa_kernel(
     with ExitStack() as ctx:
         keep = ctx.enter_context(tc.tile_pool(name="keep", bufs=1))
         rows = ctx.enter_context(tc.tile_pool(name="rows", bufs=B_TILES))
-        prep = ctx.enter_context(tc.tile_pool(name="prep", bufs=2))
+        prep = ctx.enter_context(tc.tile_pool(name="prep", bufs=3))
         work = ctx.enter_context(tc.tile_pool(name="work", bufs=3))
         stage = ctx.enter_context(tc.tile_pool(name="stage", bufs=3))
         gate_banks = ctx.enter_context(tc.psum_pool(name="gate_banks", bufs=4))
         turn_banks = ctx.enter_context(tc.psum_pool(name="turn_banks", bufs=4))
+        ctx.enter_context(tc.manual_schedule())
 
         ident = keep.tile([P, P], F32)
         make_identity(nc, ident[:])
@@ -135,12 +136,15 @@ def tile_lstmcell_pa_kernel(
         bias_cols = keep.tile([P, P], F32)
         nc.vector.tensor_copy(out=bias_cols[:], in_=bias_bank[:])
 
-        def prepare_z(bt):
-            c = bt // TILES_PER_CHUNK
-            b_cols = slice((bt % TILES_PER_CHUNK) * P, (bt % TILES_PER_CHUNK + 1) * P)
-            z_rows = prep.tile([P, H], BF16)
-            nc.vector.tensor_tensor(out=z_rows[:], in0=x_rows[bt][:], in1=h_rows[bt][:], op=ALU.add)
-            z_words = z_rows[:].bitcast(F32)
+        z_rows = {}
+        grouped = {}
+
+        def add_z(bt):
+            z_rows[bt] = prep.tile([P, H], BF16, name="z_rows")
+            nc.vector.tensor_tensor(out=z_rows[bt][:], in0=x_rows[bt][:], in1=h_rows[bt][:], op=ALU.add)
+
+        def turn_z(bt):
+            z_words = z_rows[bt][:].bitcast(F32)
             turned = turn_banks.tile([P, K_GROUPS, 2, P], F32, tag="turn")
             for g in range(K_GROUPS):
                 for u in range(2):
@@ -149,13 +153,17 @@ def tile_lstmcell_pa_kernel(
                         z_words[:, (K_PASS // 2) * g + u : (K_PASS // 2) * (g + 1) : 2],
                         ident[:],
                     )
-            grouped = prep.tile([P, K_GROUPS, P, PACK], BF16, align_bytes=64)
-            nc.vector.tensor_copy(out=grouped[:].bitcast(F32), in_=turned[:].rearrange("p g u b -> p g b u"))
+            grouped[bt] = prep.tile([P, K_GROUPS, P, PACK], BF16, align_bytes=64, name="grouped")
+            nc.scalar.copy(out=grouped[bt][:].bitcast(F32), in_=turned[:].rearrange("p g u b -> p g b u"))
+
+        def quantise_z(bt):
+            c = bt // TILES_PER_CHUNK
+            b_cols = slice((bt % TILES_PER_CHUNK) * P, (bt % TILES_PER_CHUNK + 1) * P)
             for g in range(K_GROUPS):
                 nc.vector.quantize_mx(
                     out=z_codes[c][:, g, b_cols].bitcast(FP8X4),
                     scales=z_planes[c][:, g, b_cols],
-                    in_=grouped[:, g, :, :].rearrange("p b t -> p (b t)"),
+                    in_=grouped[bt][:, g, :, :].rearrange("p b t -> p (b t)"),
                 )
 
         def gates_of(c, j):
@@ -188,10 +196,9 @@ def tile_lstmcell_pa_kernel(
 
         staged = {}
 
-        def finish(c, j, cell_t, gate_o_t):
+        def turn_back(c, j, cell_t, gate_o_t):
             if j % STEPS_PER_STORE == 0:
                 staged["c"] = stage.tile([P, TILES_PER_CHUNK, STORE_COLS], F32, name="c_stage")
-                staged["h"] = stage.tile([P, TILES_PER_CHUNK, STORE_COLS], F32, name="h_stage")
             cols = slice((j % STEPS_PER_STORE) * P, (j % STEPS_PER_STORE + 1) * P)
             c_bank = turn_banks.tile([P, TILES_PER_CHUNK, P], F32, tag="turn")
             o_bank = turn_banks.tile([P, TILES_PER_CHUNK, P], F32, tag="turn")
@@ -200,24 +207,47 @@ def tile_lstmcell_pa_kernel(
             for t in range(TILES_PER_CHUNK):
                 nc.tensor.transpose(o_bank[:, t, :], gate_o_t[:, t * P : (t + 1) * P], ident[:])
             nc.vector.tensor_copy(out=staged["c"][:, :, cols], in_=c_bank[:])
-            tanh_c = work.tile([P, TILES_PER_CHUNK, P], F32)
-            nc.scalar.activation(out=tanh_c[:], in_=staged["c"][:, :, cols], func=ACT.Tanh)
-            nc.vector.tensor_tensor(out=staged["h"][:, :, cols], in0=o_bank[:], in1=tanh_c[:], op=ALU.mult)
             if j % STEPS_PER_STORE == STEPS_PER_STORE - 1:
                 n_cols = slice((j + 1) * P - STORE_COLS, (j + 1) * P)
                 nc.sync.dma_start(out=out_view[0, c, :, :, n_cols], in_=staged["c"][:])
+            return staged["c"][:, :, cols], o_bank
+
+        def hidden(c, j, c_cols, o_bank):
+            if j % STEPS_PER_STORE == 0:
+                staged["h"] = stage.tile([P, TILES_PER_CHUNK, STORE_COLS], F32, name="h_stage")
+            cols = slice((j % STEPS_PER_STORE) * P, (j % STEPS_PER_STORE + 1) * P)
+            tanh_c = work.tile([P, TILES_PER_CHUNK, P], F32)
+            nc.scalar.activation(out=tanh_c[:], in_=c_cols, func=ACT.Tanh)
+            nc.vector.tensor_tensor(out=staged["h"][:, :, cols], in0=o_bank[:], in1=tanh_c[:], op=ALU.mult)
+            if j % STEPS_PER_STORE == STEPS_PER_STORE - 1:
+                n_cols = slice((j + 1) * P - STORE_COLS, (j + 1) * P)
                 nc.sync.dma_start(out=out_view[1, c, :, :, n_cols], in_=staged["h"][:])
 
         for bt in range(TILES_PER_CHUNK):
-            prepare_z(bt)
-        waiting = []
-        for c in range(CHUNKS):
-            for j in range(N_TILES):
-                cell_t, gate_o_t = gates_of(c, j)
-                ahead = j - Z_PREP_FIRST_STEP
-                if c + 1 < CHUNKS and 0 <= ahead < TILES_PER_CHUNK:
-                    prepare_z((c + 1) * TILES_PER_CHUNK + ahead)
-                if waiting:
-                    finish(*waiting.pop())
-                waiting.append((c, j, cell_t, gate_o_t))
-        finish(*waiting.pop())
+            add_z(bt)
+            turn_z(bt)
+            if bt > 0:
+                quantise_z(bt - 1)
+        quantise_z(TILES_PER_CHUNK - 1)
+
+        steps = [(c, j) for c in range(CHUNKS) for j in range(N_TILES)]
+        turned_gates = {}
+        turned_back = {}
+        for s in range(len(steps) + 2):
+            if s < len(steps):
+                c, j = steps[s]
+                ahead = (c + 1) * TILES_PER_CHUNK + j - Z_PREP_FIRST_STEP
+                first_ahead = (c + 1) * TILES_PER_CHUNK
+                prepare = c + 1 < CHUNKS and first_ahead <= ahead < first_ahead + TILES_PER_CHUNK
+                quantise = c + 1 < CHUNKS and first_ahead < ahead <= first_ahead + TILES_PER_CHUNK
+                if prepare:
+                    add_z(ahead)
+                turned_gates[s] = gates_of(c, j)
+                if quantise:
+                    quantise_z(ahead - 1)
+                if prepare:
+                    turn_z(ahead)
+            if 0 <= s - 1 < len(steps):
+                turned_back[s - 1] = turn_back(*steps[s - 1], *turned_gates[s - 1])
+            if 0 <= s - 2:
+                hidden(*steps[s - 2], *turned_back[s - 2])

@@ -24,8 +24,7 @@ B_CHUNK = 512
 CHUNKS = B // B_CHUNK
 TILES_PER_CHUNK = B_CHUNK // P
 PLANE_ROWS = 4
-W_PIECES = 4
-W_PIECE = H // W_PIECES
+W_RANGES = ((0, 128), (128, 256), (256, 512), (512, 768), (768, 1024))
 STEPS_PER_STORE = 2
 STORE_COLS = STEPS_PER_STORE * P
 Z_PREP_FIRST_STEP = 2
@@ -73,7 +72,7 @@ def tile_lstmcell_pa_kernel(
         ident = keep.tile([P, P], F32)
         make_identity(nc, ident[:])
 
-        w_planes = keep.tile([P, K_GROUPS, H], U8, align_bytes=64)
+        w_planes = keep.tile([P, len(GATES), K_GROUPS, H], U8, align_bytes=64)
         nc.vector.memset(w_planes[:].bitcast(I32), 0)
         bias_rows = keep.tile([P, P], BF16)
         nc.vector.memset(bias_rows[:], 0.0)
@@ -97,22 +96,22 @@ def tile_lstmcell_pa_kernel(
             h_rows.append(rows.tile([P, H], BF16, name="h_rows"))
             nc.sync.dma_start(out=h_rows[bt][:], in_=short_term_memory[b_rows, :])
 
-        def load_scales():
-            for q, gate in enumerate(GATES):
-                by_row = scales_in[gate].rearrange("g (Q r) n -> r Q g n", r=PLANE_ROWS)
-                for r in range(PLANE_ROWS):
-                    nc.sync.dma_start(
-                        out=w_planes[PLANE_ROWS * q + r : P : 32, :, :].bitcast(I32),
-                        in_=by_row[r].bitcast(I32),
-                    )
-
-        def load_words(piece):
-            for gate in GATES:
-                by_partition = words_in[gate].rearrange("g p n t -> p g (n t)")
+        def load_scales(gate):
+            q = GATES.index(gate)
+            by_row = scales_in[gate].rearrange("g (Q r) n -> r Q g n", r=PLANE_ROWS)
+            for r in range(PLANE_ROWS):
                 nc.sync.dma_start(
-                    out=w_codes[gate][:, :, piece * W_PIECE : (piece + 1) * W_PIECE].bitcast(I32),
-                    in_=by_partition[:, :, piece * W_PIECE * PACK : (piece + 1) * W_PIECE * PACK].bitcast(I32),
+                    out=w_planes[PLANE_ROWS * q + r : P : 32, q, :, :].bitcast(I32),
+                    in_=by_row[r].bitcast(I32),
                 )
+
+        def load_words(gate, piece):
+            lo, hi = W_RANGES[piece]
+            by_partition = words_in[gate].rearrange("g p n t -> p g (n t)")
+            nc.sync.dma_start(
+                out=w_codes[gate][:, :, lo:hi].bitcast(I32),
+                in_=by_partition[:, :, lo * PACK : hi * PACK].bitcast(I32),
+            )
 
         for q, gate in enumerate(GATES):
             nc.scalar.dma_start(
@@ -121,20 +120,17 @@ def tile_lstmcell_pa_kernel(
             )
         for bt in range(TILES_PER_CHUNK):
             load_rows(bt)
-        load_scales()
-        load_words(0)
-        load_words(1)
+        for gate in GATES:
+            load_scales(gate)
+            load_words(gate, 0)
+        for piece in (1, 2):
+            for gate in GATES:
+                load_words(gate, piece)
         for bt in range(TILES_PER_CHUNK, B_TILES):
             load_rows(bt)
-        load_words(2)
-        load_words(3)
-
-        bias_f32 = keep.tile([P, P], F32)
-        nc.vector.tensor_copy(out=bias_f32[:], in_=bias_rows[:])
-        bias_bank = turn_banks.tile([P, P], F32, tag="turn")
-        nc.tensor.transpose(bias_bank[:], bias_f32[:], ident[:])
-        bias_cols = keep.tile([P, P], F32)
-        nc.vector.tensor_copy(out=bias_cols[:], in_=bias_bank[:])
+        for piece in (3, 4):
+            for gate in GATES:
+                load_words(gate, piece)
 
         z_rows = {}
         grouped = {}
@@ -175,7 +171,7 @@ def tile_lstmcell_pa_kernel(
                     nc.tensor.matmul_mx(
                         out=bank[:],
                         lhsT=w_codes[gate][:, g, n_cols].bitcast(FP8X4),
-                        lhsT_scale=w_planes[PLANE_ROWS * q : P, g, n_cols],
+                        lhsT_scale=w_planes[PLANE_ROWS * q : P, q, g, n_cols],
                         rhs=z_codes[c][:, g, :].bitcast(FP8X4),
                         rhs_scale=z_planes[c][:, g, :],
                         start=(g == 0),
@@ -228,7 +224,14 @@ def tile_lstmcell_pa_kernel(
             turn_z(bt)
             if bt > 0:
                 quantise_z(bt - 1)
+
+        bias_f32 = keep.tile([P, P], F32)
+        nc.vector.tensor_copy(out=bias_f32[:], in_=bias_rows[:])
+        bias_bank = turn_banks.tile([P, P], F32, tag="turn")
+        nc.tensor.transpose(bias_bank[:], bias_f32[:], ident[:])
         quantise_z(TILES_PER_CHUNK - 1)
+        bias_cols = keep.tile([P, P], F32)
+        nc.vector.tensor_copy(out=bias_cols[:], in_=bias_bank[:])
 
         steps = [(c, j) for c in range(CHUNKS) for j in range(N_TILES)]
         turned_gates = {}

@@ -135,27 +135,39 @@ def tile_lstmcell_pa_kernel(
         z_rows = {}
         grouped = {}
 
-        def add_z(bt):
-            z_rows[bt] = prep.tile([P, H], BF16, name="z_rows")
-            nc.vector.tensor_tensor(out=z_rows[bt][:], in0=x_rows[bt][:], in1=h_rows[bt][:], op=ALU.add)
+        def halves_of(part):
+            return range(K_GROUPS) if part is None else (part,)
 
-        def turn_z(bt):
+        def add_z(bt, part=None):
+            if part is None or part == 0:
+                z_rows[bt] = prep.tile([P, H], BF16, name="z_rows")
+            k_cols = slice(halves_of(part)[0] * K_PASS, (halves_of(part)[-1] + 1) * K_PASS)
+            nc.vector.tensor_tensor(
+                out=z_rows[bt][:, k_cols], in0=x_rows[bt][:, k_cols], in1=h_rows[bt][:, k_cols], op=ALU.add
+            )
+
+        def turn_z(bt, part=None):
             z_words = z_rows[bt][:].bitcast(F32)
-            turned = turn_banks.tile([P, K_GROUPS, 2, P], F32, tag="turn")
-            for g in range(K_GROUPS):
+            passes = halves_of(part)
+            turned = turn_banks.tile([P, len(passes), 2, P], F32, tag="turn")
+            for at, g in enumerate(passes):
                 for u in range(2):
                     nc.tensor.transpose(
-                        turned[:, g, u, :],
+                        turned[:, at, u, :],
                         z_words[:, (K_PASS // 2) * g + u : (K_PASS // 2) * (g + 1) : 2],
                         ident[:],
                     )
-            grouped[bt] = prep.tile([P, K_GROUPS, P, PACK], BF16, align_bytes=64, name="grouped")
-            nc.scalar.copy(out=grouped[bt][:].bitcast(F32), in_=turned[:].rearrange("p g u b -> p g b u"))
+            if part is None or part == 0:
+                grouped[bt] = prep.tile([P, K_GROUPS, P, PACK], BF16, align_bytes=64, name="grouped")
+            nc.scalar.copy(
+                out=grouped[bt][:, passes[0] : passes[-1] + 1, :, :].bitcast(F32),
+                in_=turned[:].rearrange("p g u b -> p g b u"),
+            )
 
-        def quantise_z(bt):
+        def quantise_z(bt, part=None):
             c = bt // TILES_PER_CHUNK
             b_cols = slice((bt % TILES_PER_CHUNK) * P, (bt % TILES_PER_CHUNK + 1) * P)
-            for g in range(K_GROUPS):
+            for g in halves_of(part):
                 nc.vector.quantize_mx(
                     out=z_codes[c][:, g, b_cols].bitcast(FP8X4),
                     scales=z_planes[c][:, g, b_cols],
@@ -191,6 +203,15 @@ def tile_lstmcell_pa_kernel(
             return cell_t, acts["o"]
 
         staged = {}
+        last_step = (CHUNKS - 1, N_TILES - 1)
+
+        def store(which, o, c, j):
+            if c == CHUNKS - 1 and j >= N_TILES - STEPS_PER_STORE:
+                cols = slice((j % STEPS_PER_STORE) * P, (j % STEPS_PER_STORE + 1) * P)
+                nc.sync.dma_start(out=out_view[o, c, :, :, j * P : (j + 1) * P], in_=staged[which][:, :, cols])
+            elif j % STEPS_PER_STORE == STEPS_PER_STORE - 1:
+                n_cols = slice((j + 1) * P - STORE_COLS, (j + 1) * P)
+                nc.sync.dma_start(out=out_view[o, c, :, :, n_cols], in_=staged[which][:])
 
         def turn_back(c, j, cell_t, gate_o_t):
             if j % STEPS_PER_STORE == 0:
@@ -202,10 +223,10 @@ def tile_lstmcell_pa_kernel(
                 nc.tensor.transpose(c_bank[:, t, :], cell_t[:, t * P : (t + 1) * P], ident[:])
             for t in range(TILES_PER_CHUNK):
                 nc.tensor.transpose(o_bank[:, t, :], gate_o_t[:, t * P : (t + 1) * P], ident[:])
+            if (c, j) == last_step:
+                return c_bank[:], o_bank
             nc.vector.tensor_copy(out=staged["c"][:, :, cols], in_=c_bank[:])
-            if j % STEPS_PER_STORE == STEPS_PER_STORE - 1:
-                n_cols = slice((j + 1) * P - STORE_COLS, (j + 1) * P)
-                nc.sync.dma_start(out=out_view[0, c, :, :, n_cols], in_=staged["c"][:])
+            store("c", 0, c, j)
             return staged["c"][:, :, cols], o_bank
 
         def hidden(c, j, c_cols, o_bank):
@@ -214,24 +235,32 @@ def tile_lstmcell_pa_kernel(
             cols = slice((j % STEPS_PER_STORE) * P, (j % STEPS_PER_STORE + 1) * P)
             tanh_c = work.tile([P, TILES_PER_CHUNK, P], F32)
             nc.scalar.activation(out=tanh_c[:], in_=c_cols, func=ACT.Tanh)
+            if (c, j) == last_step:
+                nc.scalar.copy(out=staged["c"][:, :, cols], in_=c_cols)
+                store("c", 0, c, j)
             nc.vector.tensor_tensor(out=staged["h"][:, :, cols], in0=o_bank[:], in1=tanh_c[:], op=ALU.mult)
-            if j % STEPS_PER_STORE == STEPS_PER_STORE - 1:
-                n_cols = slice((j + 1) * P - STORE_COLS, (j + 1) * P)
-                nc.sync.dma_start(out=out_view[1, c, :, :, n_cols], in_=staged["h"][:])
+            store("h", 1, c, j)
 
-        for bt in range(TILES_PER_CHUNK):
+        last_tile = TILES_PER_CHUNK - 1
+        bias_f32 = keep.tile([P, P], F32)
+        bias_cols = keep.tile([P, P], F32)
+        bias_bank = None
+        for bt in range(last_tile):
             add_z(bt)
             turn_z(bt)
+            if bt == last_tile - 1:
+                nc.vector.tensor_copy(out=bias_f32[:], in_=bias_rows[:])
+                bias_bank = turn_banks.tile([P, P], F32, tag="turn", name="bias_bank")
+                nc.tensor.transpose(bias_bank[:], bias_f32[:], ident[:])
             if bt > 0:
                 quantise_z(bt - 1)
-
-        bias_f32 = keep.tile([P, P], F32)
-        nc.vector.tensor_copy(out=bias_f32[:], in_=bias_rows[:])
-        bias_bank = turn_banks.tile([P, P], F32, tag="turn")
-        nc.tensor.transpose(bias_bank[:], bias_f32[:], ident[:])
-        quantise_z(TILES_PER_CHUNK - 1)
-        bias_cols = keep.tile([P, P], F32)
+        for g in range(K_GROUPS):
+            add_z(last_tile, g)
+            turn_z(last_tile, g)
         nc.vector.tensor_copy(out=bias_cols[:], in_=bias_bank[:])
+        quantise_z(last_tile - 1)
+        for g in range(K_GROUPS):
+            quantise_z(last_tile, g)
 
         steps = [(c, j) for c in range(CHUNKS) for j in range(N_TILES)]
         turned_gates = {}

@@ -27,6 +27,7 @@ PLANE_ROWS = 4
 W_RANGES = ((0, 128), (128, 256), (256, 512), (512, 768), (768, 1024))
 STEPS_PER_STORE = 2
 STORE_COLS = STEPS_PER_STORE * P
+IDLE_MATMULS = (2, 2, 2, 1, 3)
 Z_PREP_FIRST_STEP = 2
 
 GATES = ("i", "g", "f", "o")
@@ -242,6 +243,9 @@ def tile_lstmcell_pa_kernel(
             store("h", 1, c, j)
 
         last_tile = TILES_PER_CHUNK - 1
+        idle_in = keep.tile([P, B_CHUNK], BF16)
+        nc.gpsimd.memset(idle_in[:], 0.0)
+        idle_bank = gate_banks.tile([P, B_CHUNK], F32, tag="gate", name="idle_bank")
         bias_f32 = keep.tile([P, P], F32)
         bias_cols = keep.tile([P, P], F32)
         bias_bank = None
@@ -252,11 +256,15 @@ def tile_lstmcell_pa_kernel(
                 nc.vector.tensor_copy(out=bias_f32[:], in_=bias_rows[:])
                 bias_bank = turn_banks.tile([P, P], F32, tag="turn", name="bias_bank")
                 nc.tensor.transpose(bias_bank[:], bias_f32[:], ident[:])
+            for rep in range(IDLE_MATMULS[bt]):
+                nc.tensor.matmul(out=idle_bank[:], lhsT=idle_in[:, 0:P], rhs=idle_in[:], start=True, stop=True)
             if bt > 0:
                 quantise_z(bt - 1)
         for g in range(K_GROUPS):
             add_z(last_tile, g)
             turn_z(last_tile, g)
+            for rep in range(IDLE_MATMULS[last_tile + g]):
+                nc.tensor.matmul(out=idle_bank[:], lhsT=idle_in[:, 0:P], rhs=idle_in[:], start=True, stop=True)
         nc.vector.tensor_copy(out=bias_cols[:], in_=bias_bank[:])
         quantise_z(last_tile - 1)
         for g in range(K_GROUPS):

@@ -142,10 +142,15 @@ def tile_lstmcell_pa_kernel(
         def add_z(bt, part=None):
             if part is None or part == 0:
                 z_rows[bt] = prep.tile([P, H], BF16, name="z_rows")
-            k_cols = slice(halves_of(part)[0] * K_PASS, (halves_of(part)[-1] + 1) * K_PASS)
-            nc.vector.tensor_tensor(
-                out=z_rows[bt][:, k_cols], in0=x_rows[bt][:, k_cols], in1=h_rows[bt][:, k_cols], op=ALU.add
-            )
+            in_order = "p (g q u e) -> p g u q e"
+            out_order = "p (g u q e) -> p g u q e"
+            for g in halves_of(part):
+                nc.vector.tensor_tensor(
+                    out=z_rows[bt][:].rearrange(out_order, g=K_GROUPS, u=2, e=2)[:, g],
+                    in0=x_rows[bt][:].rearrange(in_order, g=K_GROUPS, u=2, e=2)[:, g],
+                    in1=h_rows[bt][:].rearrange(in_order, g=K_GROUPS, u=2, e=2)[:, g],
+                    op=ALU.add,
+                )
 
         def turn_z(bt, part=None):
             z_words = z_rows[bt][:].bitcast(F32)
@@ -155,7 +160,7 @@ def tile_lstmcell_pa_kernel(
                 for u in range(2):
                     nc.tensor.transpose(
                         turned[:, at, u, :],
-                        z_words[:, (K_PASS // 2) * g + u : (K_PASS // 2) * (g + 1) : 2],
+                        z_words[:, (K_PASS // 2) * g + P * u : (K_PASS // 2) * g + P * (u + 1)],
                         ident[:],
                     )
             if part is None or part == 0:

@@ -27,6 +27,7 @@ PLANE_ROWS = 4
 W_RANGES = ((0, 128), (128, 256), (256, 512), (512, 768), (768, 1024))
 STEPS_PER_STORE = 2
 STORE_COLS = STEPS_PER_STORE * P
+BRIDGE_COLS = 64
 IDLE_MATMULS = (2, 2, 2, 1, 3)
 Z_PREP_FIRST_STEP = 2
 
@@ -70,6 +71,10 @@ def tile_lstmcell_pa_kernel(
         turn_banks = ctx.enter_context(tc.psum_pool(name="turn_banks", bufs=4))
         ctx.enter_context(tc.manual_schedule())
 
+        first_in = keep.tile([P, 1], F32)
+        nc.gpsimd.memset(first_in[:], 0.0)
+        first_out = keep.tile([P, 1], F32)
+        nc.scalar.activation(out=first_out[:], in_=first_in[:], func=ACT.Sigmoid)
         ident = keep.tile([P, P], F32)
         make_identity(nc, ident[:])
 
@@ -152,10 +157,15 @@ def tile_lstmcell_pa_kernel(
                     op=ALU.add,
                 )
 
-        def turn_z(bt, part=None):
+        def bridge(bank_cols):
+            nc.tensor.matmul(out=bank_cols, lhsT=idle_in[:, 0:P], rhs=idle_in[:, 0:BRIDGE_COLS], start=True, stop=True)
+
+        def turn_z(bt, part=None, after_passes=False):
             z_words = z_rows[bt][:].bitcast(F32)
             passes = halves_of(part)
             turned = turn_banks.tile([P, len(passes), 2, P], F32, tag="turn")
+            if after_passes:
+                bridge(turned[:, 0, 0, 0:BRIDGE_COLS])
             for at, g in enumerate(passes):
                 for u in range(2):
                     nc.tensor.transpose(
@@ -180,11 +190,13 @@ def tile_lstmcell_pa_kernel(
                     in_=grouped[bt][:, g, :, :].rearrange("p b t -> p (b t)"),
                 )
 
-        def gates_of(c, j):
+        def gates_of(c, j, after_transposes):
             n_cols = slice(j * P, (j + 1) * P)
             acts = {}
             for q, gate in enumerate(GATES):
                 bank = gate_banks.tile([P, B_CHUNK], F32, tag="gate")
+                if after_transposes and q == 0:
+                    bridge(bank[:, 0:BRIDGE_COLS])
                 for g in range(K_GROUPS):
                     nc.tensor.matmul_mx(
                         out=bank[:],
@@ -219,12 +231,14 @@ def tile_lstmcell_pa_kernel(
                 n_cols = slice((j + 1) * P - STORE_COLS, (j + 1) * P)
                 nc.sync.dma_start(out=out_view[o, c, :, :, n_cols], in_=staged[which][:])
 
-        def turn_back(c, j, cell_t, gate_o_t):
+        def turn_back(c, j, cell_t, gate_o_t, after_passes):
             if j % STEPS_PER_STORE == 0:
                 staged["c"] = stage.tile([P, TILES_PER_CHUNK, STORE_COLS], F32, name="c_stage")
             cols = slice((j % STEPS_PER_STORE) * P, (j % STEPS_PER_STORE + 1) * P)
             c_bank = turn_banks.tile([P, TILES_PER_CHUNK, P], F32, tag="turn")
             o_bank = turn_banks.tile([P, TILES_PER_CHUNK, P], F32, tag="turn")
+            if after_passes:
+                bridge(c_bank[:, 0, 0:BRIDGE_COLS])
             for t in range(TILES_PER_CHUNK):
                 nc.tensor.transpose(c_bank[:, t, :], cell_t[:, t * P : (t + 1) * P], ident[:])
             for t in range(TILES_PER_CHUNK):
@@ -287,12 +301,16 @@ def tile_lstmcell_pa_kernel(
                 quantise = c + 1 < CHUNKS and first_ahead < ahead <= first_ahead + TILES_PER_CHUNK
                 if prepare:
                     add_z(ahead)
-                turned_gates[s] = gates_of(c, j)
+                turned_gates[s] = gates_of(c, j, after_transposes=s > 1)
                 if quantise:
                     quantise_z(ahead - 1)
                 if prepare:
-                    turn_z(ahead)
+                    turn_z(ahead, after_passes=True)
+            else:
+                prepare = False
             if 0 <= s - 1 < len(steps):
-                turned_back[s - 1] = turn_back(*steps[s - 1], *turned_gates[s - 1])
+                turned_back[s - 1] = turn_back(
+                    *steps[s - 1], *turned_gates[s - 1], after_passes=s < len(steps) and not prepare
+                )
             if 0 <= s - 2:
                 hidden(*steps[s - 2], *turned_back[s - 2])

@@ -27,7 +27,7 @@ PLANE_ROWS = 4
 W_RANGES = ((0, 128), (128, 256), (256, 512), (512, 768), (768, 1024))
 STEPS_PER_STORE = 2
 STORE_COLS = STEPS_PER_STORE * P
-BRIDGE_COLS = 64
+BRIDGE_COLS = 32
 IDLE_MATMULS = (2, 2, 2, 1, 3)
 Z_PREP_FIRST_STEP = 2
 

@@ -24,10 +24,11 @@ B_CHUNK = 512
 CHUNKS = B // B_CHUNK
 TILES_PER_CHUNK = B_CHUNK // P
 PLANE_ROWS = 4
-W_RANGES = ((0, 128), (128, 256), (256, 512), (512, 768), (768, 1024))
+W_RANGES = ((0, 256), (256, 512), (512, 768), (768, 1024))
 STEPS_PER_STORE = 2
 STORE_COLS = STEPS_PER_STORE * P
 BRIDGE_COLS = 32
+HALF_ROWS = 256
 IDLE_MATMULS = (2, 2, 2, 1, 3)
 Z_PREP_FIRST_STEP = 2
 
@@ -66,7 +67,7 @@ def tile_lstmcell_pa_kernel(
         rows = ctx.enter_context(tc.tile_pool(name="rows", bufs=B_TILES))
         prep = ctx.enter_context(tc.tile_pool(name="prep", bufs=3))
         work = ctx.enter_context(tc.tile_pool(name="work", bufs=3))
-        stage = ctx.enter_context(tc.tile_pool(name="stage", bufs=3))
+        stage = ctx.enter_context(tc.tile_pool(name="stage", bufs=4))
         gate_banks = ctx.enter_context(tc.psum_pool(name="gate_banks", bufs=4))
         turn_banks = ctx.enter_context(tc.psum_pool(name="turn_banks", bufs=4))
         ctx.enter_context(tc.manual_schedule())
@@ -129,12 +130,11 @@ def tile_lstmcell_pa_kernel(
         for gate in GATES:
             load_scales(gate)
             load_words(gate, 0)
-        for piece in (1, 2):
-            for gate in GATES:
-                load_words(gate, piece)
+        for gate in GATES:
+            load_words(gate, 1)
         for bt in range(TILES_PER_CHUNK, B_TILES):
             load_rows(bt)
-        for piece in (3, 4):
+        for piece in (2, 3):
             for gate in GATES:
                 load_words(gate, piece)
 
@@ -190,76 +190,95 @@ def tile_lstmcell_pa_kernel(
                     in_=grouped[bt][:, g, :, :].rearrange("p b t -> p (b t)"),
                 )
 
-        def gates_of(c, j, after_transposes):
-            n_cols = slice(j * P, (j + 1) * P)
+        def gates_of(group, after_transposes):
             acts = {}
             for q, gate in enumerate(GATES):
-                bank = gate_banks.tile([P, B_CHUNK], F32, tag="gate")
-                if after_transposes and q == 0:
-                    bridge(bank[:, 0:BRIDGE_COLS])
-                for g in range(K_GROUPS):
-                    nc.tensor.matmul_mx(
-                        out=bank[:],
-                        lhsT=w_codes[gate][:, g, n_cols].bitcast(FP8X4),
-                        lhsT_scale=w_planes[PLANE_ROWS * q : P, q, g, n_cols],
-                        rhs=z_codes[c][:, g, :].bitcast(FP8X4),
-                        rhs_scale=z_planes[c][:, g, :],
-                        start=(g == 0),
-                        stop=(g == K_GROUPS - 1),
+                for b0, nb, j in group:
+                    n_cols = slice(j * P, (j + 1) * P)
+                    c = b0 // B_CHUNK
+                    b_cols = slice(b0 % B_CHUNK, b0 % B_CHUNK + nb)
+                    bank = gate_banks.tile([P, B_CHUNK], F32, tag="gate")
+                    if after_transposes and q == 0:
+                        bridge(bank[:, 0:BRIDGE_COLS])
+                    for g in range(K_GROUPS):
+                        nc.tensor.matmul_mx(
+                            out=bank[:, 0:nb],
+                            lhsT=w_codes[gate][:, g, n_cols].bitcast(FP8X4),
+                            lhsT_scale=w_planes[PLANE_ROWS * q : P, q, g, n_cols],
+                            rhs=z_codes[c][:, g, b_cols].bitcast(FP8X4),
+                            rhs_scale=z_planes[c][:, g, b_cols],
+                            start=(g == 0),
+                            stop=(g == K_GROUPS - 1),
+                        )
+                    acts[gate, b0, j] = work.tile([P, nb], F32, name="act_" + gate)
+                    nc.scalar.activation(
+                        out=acts[gate, b0, j][:],
+                        in_=bank[:, 0:nb],
+                        func=GATE_FUNC[gate],
+                        bias=bias_cols[:, N_TILES * q + j : N_TILES * q + j + 1],
+                        scale=1.0,
                     )
-                acts[gate] = work.tile([P, B_CHUNK], F32, name="act_" + gate)
-                nc.scalar.activation(
-                    out=acts[gate][:],
-                    in_=bank[:],
-                    func=GATE_FUNC[gate],
-                    bias=bias_cols[:, N_TILES * q + j : N_TILES * q + j + 1],
-                    scale=1.0,
-                )
-            cell_t = work.tile([P, B_CHUNK], F32)
-            nc.vector.tensor_tensor(out=cell_t[:], in0=acts["i"][:], in1=acts["g"][:], op=ALU.mult)
-            nc.vector.tensor_tensor(out=cell_t[:], in0=cell_t[:], in1=acts["f"][:], op=ALU.add)
-            return cell_t, acts["o"]
+            cells = {}
+            for b0, nb, j in group:
+                cells[b0, j] = work.tile([P, nb], F32, name="cell_t")
+                nc.vector.tensor_tensor(out=cells[b0, j][:], in0=acts["i", b0, j][:], in1=acts["g", b0, j][:], op=ALU.mult)
+            for b0, nb, j in group:
+                nc.vector.tensor_tensor(out=cells[b0, j][:], in0=cells[b0, j][:], in1=acts["f", b0, j][:], op=ALU.add)
+            return [(cells[b0, j], acts["o", b0, j]) for b0, nb, j in group]
 
         staged = {}
-        last_step = (CHUNKS - 1, N_TILES - 1)
 
-        def store(which, o, c, j):
+        def stage_cols(j):
+            return slice((j % STEPS_PER_STORE) * P, (j % STEPS_PER_STORE + 1) * P)
+
+        def stage_for(which, step):
+            b0, nb, j = step
+            if j % STEPS_PER_STORE == 0 or nb < B_CHUNK:
+                staged[which] = stage.tile([P, nb // P, STORE_COLS], F32, name=which + "_stage")
+
+        def store(which, o, step):
+            b0, nb, j = step
+            c = b0 // B_CHUNK
+            tiles = slice(b0 % B_CHUNK // P, (b0 % B_CHUNK + nb) // P)
             if c == CHUNKS - 1 and j >= N_TILES - STEPS_PER_STORE:
-                cols = slice((j % STEPS_PER_STORE) * P, (j % STEPS_PER_STORE + 1) * P)
-                nc.sync.dma_start(out=out_view[o, c, :, :, j * P : (j + 1) * P], in_=staged[which][:, :, cols])
+                nc.sync.dma_start(out=out_view[o, c, :, tiles, j * P : (j + 1) * P], in_=staged[which][:, :, stage_cols(j)])
             elif j % STEPS_PER_STORE == STEPS_PER_STORE - 1:
                 n_cols = slice((j + 1) * P - STORE_COLS, (j + 1) * P)
-                nc.sync.dma_start(out=out_view[o, c, :, :, n_cols], in_=staged[which][:])
+                nc.sync.dma_start(out=out_view[o, c, :, tiles, n_cols], in_=staged[which][:])
 
-        def turn_back(c, j, cell_t, gate_o_t, after_passes):
-            if j % STEPS_PER_STORE == 0:
-                staged["c"] = stage.tile([P, TILES_PER_CHUNK, STORE_COLS], F32, name="c_stage")
-            cols = slice((j % STEPS_PER_STORE) * P, (j % STEPS_PER_STORE + 1) * P)
-            c_bank = turn_banks.tile([P, TILES_PER_CHUNK, P], F32, tag="turn")
-            o_bank = turn_banks.tile([P, TILES_PER_CHUNK, P], F32, tag="turn")
+        def turn_back(step, last, cell_t, gate_o_t, after_passes):
+            b0, nb, j = step
+            stage_for("c", step)
+            if nb == B_CHUNK:
+                whole_c = turn_banks.tile([P, nb // P, P], F32, tag="turn")
+                whole_o = turn_banks.tile([P, nb // P, P], F32, tag="turn")
+                c_bank, o_bank = whole_c[:], whole_o[:]
+            else:
+                both = turn_banks.tile([P, 2, nb // P, P], F32, tag="turn", name="both")
+                c_bank, o_bank = both[:, 0], both[:, 1]
             if after_passes:
                 bridge(c_bank[:, 0, 0:BRIDGE_COLS])
-            for t in range(TILES_PER_CHUNK):
+            for t in range(nb // P):
                 nc.tensor.transpose(c_bank[:, t, :], cell_t[:, t * P : (t + 1) * P], ident[:])
-            for t in range(TILES_PER_CHUNK):
+            for t in range(nb // P):
                 nc.tensor.transpose(o_bank[:, t, :], gate_o_t[:, t * P : (t + 1) * P], ident[:])
-            if (c, j) == last_step:
-                return c_bank[:], o_bank
-            nc.vector.tensor_copy(out=staged["c"][:, :, cols], in_=c_bank[:])
-            store("c", 0, c, j)
-            return staged["c"][:, :, cols], o_bank
+            if last:
+                return c_bank, o_bank
+            c_cols = staged["c"][:, :, stage_cols(j)]
+            nc.vector.tensor_copy(out=c_cols, in_=c_bank)
+            store("c", 0, step)
+            return c_cols, o_bank
 
-        def hidden(c, j, c_cols, o_bank):
-            if j % STEPS_PER_STORE == 0:
-                staged["h"] = stage.tile([P, TILES_PER_CHUNK, STORE_COLS], F32, name="h_stage")
-            cols = slice((j % STEPS_PER_STORE) * P, (j % STEPS_PER_STORE + 1) * P)
-            tanh_c = work.tile([P, TILES_PER_CHUNK, P], F32)
+        def hidden(step, last, c_cols, o_bank):
+            b0, nb, j = step
+            stage_for("h", step)
+            tanh_c = work.tile([P, nb // P, P], F32, name="tanh_c")
             nc.scalar.activation(out=tanh_c[:], in_=c_cols, func=ACT.Tanh)
-            if (c, j) == last_step:
-                nc.scalar.copy(out=staged["c"][:, :, cols], in_=c_cols)
-                store("c", 0, c, j)
-            nc.vector.tensor_tensor(out=staged["h"][:, :, cols], in0=o_bank[:], in1=tanh_c[:], op=ALU.mult)
-            store("h", 1, c, j)
+            if last:
+                nc.scalar.copy(out=staged["c"][:, :, stage_cols(j)], in_=c_cols)
+                store("c", 0, step)
+            nc.vector.tensor_tensor(out=staged["h"][:, :, stage_cols(j)], in0=o_bank, in1=tanh_c[:], op=ALU.mult)
+            store("h", 1, step)
 
         last_tile = TILES_PER_CHUNK - 1
         idle_in = keep.tile([P, B_CHUNK], BF16)
@@ -289,28 +308,32 @@ def tile_lstmcell_pa_kernel(
         for g in range(K_GROUPS):
             quantise_z(last_tile, g)
 
-        steps = [(c, j) for c in range(CHUNKS) for j in range(N_TILES)]
+        steps = [(c * B_CHUNK, B_CHUNK, j) for c in range(CHUNKS) for j in range(N_TILES)]
+        steps[-1:] = [(b0, HALF_ROWS, N_TILES - 1) for b0 in (B_CHUNK, B_CHUNK + HALF_ROWS)]
+        first_group = 2
         turned_gates = {}
         turned_back = {}
         for s in range(len(steps) + 2):
+            prepare = False
             if s < len(steps):
-                c, j = steps[s]
-                ahead = (c + 1) * TILES_PER_CHUNK + j - Z_PREP_FIRST_STEP
-                first_ahead = (c + 1) * TILES_PER_CHUNK
-                prepare = c + 1 < CHUNKS and first_ahead <= ahead < first_ahead + TILES_PER_CHUNK
-                quantise = c + 1 < CHUNKS and first_ahead < ahead <= first_ahead + TILES_PER_CHUNK
+                b0, nb, j = steps[s]
+                ahead = TILES_PER_CHUNK + j - Z_PREP_FIRST_STEP
+                prepare = b0 == 0 and TILES_PER_CHUNK <= ahead < B_TILES
+                quantise = b0 == 0 and TILES_PER_CHUNK < ahead <= B_TILES
                 if prepare:
                     add_z(ahead)
-                turned_gates[s] = gates_of(c, j, after_transposes=s > 1)
+                if s == 0:
+                    for at, result in enumerate(gates_of(steps[:first_group], False)):
+                        turned_gates[at] = result
+                elif s >= first_group:
+                    turned_gates[s] = gates_of(steps[s : s + 1], s > 1)[0]
                 if quantise:
                     quantise_z(ahead - 1)
                 if prepare:
                     turn_z(ahead, after_passes=True)
-            else:
-                prepare = False
             if 0 <= s - 1 < len(steps):
                 turned_back[s - 1] = turn_back(
-                    *steps[s - 1], *turned_gates[s - 1], after_passes=s < len(steps) and not prepare
+                    steps[s - 1], s == len(steps), *turned_gates[s - 1], after_passes=s < len(steps) and not prepare
                 )
             if 0 <= s - 2:
-                hidden(*steps[s - 2], *turned_back[s - 2])
+                hidden(steps[s - 2], s - 1 == len(steps), *turned_back[s - 2])

@@ -29,7 +29,7 @@ STEPS_PER_STORE = 2
 STORE_COLS = STEPS_PER_STORE * P
 BRIDGE_COLS = 32
 HALF_ROWS = 256
-IDLE_MATMULS = (2, 2, 2, 1, 3)
+IDLE_MATMULS = (2, 2, 2, 3)
 Z_PREP_FIRST_STEP = 2
 
 GATES = ("i", "g", "f", "o")
@@ -72,6 +72,13 @@ def tile_lstmcell_pa_kernel(
         turn_banks = ctx.enter_context(tc.psum_pool(name="turn_banks", bufs=4))
         ctx.enter_context(tc.manual_schedule())
 
+        bias_rows = keep.tile([P, P], BF16)
+        nc.gpsimd.memset(bias_rows[:], 0.0)
+        for q, gate in enumerate(GATES):
+            nc.scalar.dma_start(
+                out=bias_rows[N_TILES * q : N_TILES * (q + 1), :],
+                in_=bias_in[gate].rearrange("(j n) -> j n", n=P),
+            )
         first_in = keep.tile([P, 1], F32)
         nc.gpsimd.memset(first_in[:], 0.0)
         first_out = keep.tile([P, 1], F32)
@@ -81,8 +88,6 @@ def tile_lstmcell_pa_kernel(
 
         w_planes = keep.tile([P, len(GATES), K_GROUPS, H], U8, align_bytes=64)
         nc.vector.memset(w_planes[:].bitcast(I32), 0)
-        bias_rows = keep.tile([P, P], BF16)
-        nc.vector.memset(bias_rows[:], 0.0)
 
         w_codes = {}
         for gate in GATES:
@@ -120,11 +125,6 @@ def tile_lstmcell_pa_kernel(
                 in_=by_partition[:, :, lo * PACK : hi * PACK].bitcast(I32),
             )
 
-        for q, gate in enumerate(GATES):
-            nc.scalar.dma_start(
-                out=bias_rows[N_TILES * q : N_TILES * (q + 1), :],
-                in_=bias_in[gate].rearrange("(j n) -> j n", n=P),
-            )
         for bt in range(TILES_PER_CHUNK):
             load_rows(bt)
         for gate in GATES:
@@ -190,6 +190,8 @@ def tile_lstmcell_pa_kernel(
                     in_=grouped[bt][:, g, :, :].rearrange("p b t -> p (b t)"),
                 )
 
+        open_cells = []
+
         def gates_of(group, after_transposes):
             acts = {}
             for q, gate in enumerate(GATES):
@@ -222,8 +224,14 @@ def tile_lstmcell_pa_kernel(
             for b0, nb, j in group:
                 cells[b0, j] = work.tile([P, nb], F32, name="cell_t")
                 nc.vector.tensor_tensor(out=cells[b0, j][:], in0=acts["i", b0, j][:], in1=acts["g", b0, j][:], op=ALU.mult)
-            for b0, nb, j in group:
-                nc.vector.tensor_tensor(out=cells[b0, j][:], in0=cells[b0, j][:], in1=acts["f", b0, j][:], op=ALU.add)
+            def add_f():
+                for b0, nb, j in group:
+                    nc.vector.tensor_tensor(out=cells[b0, j][:], in0=cells[b0, j][:], in1=acts["f", b0, j][:], op=ALU.add)
+
+            if len(group) > 1:
+                add_f()
+            else:
+                open_cells.append(add_f)
             return [(cells[b0, j], acts["o", b0, j]) for b0, nb, j in group]
 
         staged = {}
@@ -286,25 +294,24 @@ def tile_lstmcell_pa_kernel(
         idle_bank = gate_banks.tile([P, B_CHUNK], F32, tag="gate", name="idle_bank")
         bias_f32 = keep.tile([P, P], F32)
         bias_cols = keep.tile([P, P], F32)
-        bias_bank = None
         for bt in range(last_tile):
             add_z(bt)
             turn_z(bt)
-            if bt == last_tile - 1:
-                nc.vector.tensor_copy(out=bias_f32[:], in_=bias_rows[:])
-                bias_bank = turn_banks.tile([P, P], F32, tag="turn", name="bias_bank")
-                nc.tensor.transpose(bias_bank[:], bias_f32[:], ident[:])
             for rep in range(IDLE_MATMULS[bt]):
                 nc.tensor.matmul(out=idle_bank[:], lhsT=idle_in[:, 0:P], rhs=idle_in[:], start=True, stop=True)
-            if bt > 0:
-                quantise_z(bt - 1)
+            if bt == 1:
+                quantise_z(0)
         for g in range(K_GROUPS):
             add_z(last_tile, g)
             turn_z(last_tile, g)
-            for rep in range(IDLE_MATMULS[last_tile + g]):
-                nc.tensor.matmul(out=idle_bank[:], lhsT=idle_in[:, 0:P], rhs=idle_in[:], start=True, stop=True)
+        nc.vector.tensor_copy(out=bias_f32[:], in_=bias_rows[:])
+        bias_bank = turn_banks.tile([P, P], F32, tag="turn", name="bias_bank")
+        nc.tensor.transpose(bias_bank[:], bias_f32[:], ident[:])
+        for rep in range(IDLE_MATMULS[last_tile]):
+            nc.tensor.matmul(out=idle_bank[:], lhsT=idle_in[:, 0:P], rhs=idle_in[:], start=True, stop=True)
+        quantise_z(1)
+        quantise_z(2)
         nc.vector.tensor_copy(out=bias_cols[:], in_=bias_bank[:])
-        quantise_z(last_tile - 1)
         for g in range(K_GROUPS):
             quantise_z(last_tile, g)
 
@@ -335,5 +342,8 @@ def tile_lstmcell_pa_kernel(
                 turned_back[s - 1] = turn_back(
                     steps[s - 1], s == len(steps), *turned_gates[s - 1], after_passes=s < len(steps) and not prepare
                 )
+            for add_f in open_cells:
+                add_f()
+            open_cells.clear()
             if 0 <= s - 2:
                 hidden(steps[s - 2], s - 1 == len(steps), *turned_back[s - 2])

@@ -24,13 +24,14 @@ B_CHUNK = 512
 CHUNKS = B // B_CHUNK
 TILES_PER_CHUNK = B_CHUNK // P
 PLANE_ROWS = 4
-W_RANGES = ((0, 256), (256, 512), (512, 768), (768, 1024))
+LOAD_COLS = 256
 STEPS_PER_STORE = 2
 STORE_COLS = STEPS_PER_STORE * P
 BRIDGE_COLS = 32
 HALF_ROWS = 256
+FIRST_GROUP = LOAD_COLS // P
 IDLE_MATMULS = (2, 2, 2, 3)
-Z_PREP_FIRST_STEP = 2
+Z_FIRST_STEP = FIRST_GROUP
 
 GATES = ("i", "g", "f", "o")
 GATE_FUNC = {"i": ACT.Sigmoid, "g": ACT.Tanh, "f": ACT.Sigmoid, "o": ACT.Sigmoid}
@@ -118,7 +119,7 @@ def tile_lstmcell_pa_kernel(
                 )
 
         def load_words(gate, piece):
-            lo, hi = W_RANGES[piece]
+            lo, hi = piece * LOAD_COLS, (piece + 1) * LOAD_COLS
             by_partition = words_in[gate].rearrange("g p n t -> p g (n t)")
             nc.sync.dma_start(
                 out=w_codes[gate][:, :, lo:hi].bitcast(I32),
@@ -134,7 +135,7 @@ def tile_lstmcell_pa_kernel(
             load_words(gate, 1)
         for bt in range(TILES_PER_CHUNK, B_TILES):
             load_rows(bt)
-        for piece in (2, 3):
+        for piece in range(2, H // LOAD_COLS):
             for gate in GATES:
                 load_words(gate, piece)
 
@@ -160,11 +161,13 @@ def tile_lstmcell_pa_kernel(
         def bridge(bank_cols):
             nc.tensor.matmul(out=bank_cols, lhsT=idle_in[:, 0:P], rhs=idle_in[:, 0:BRIDGE_COLS], start=True, stop=True)
 
-        def turn_z(bt, part=None, after_passes=False):
+        def turn_z(bt, part=None):
+            second_chunk = bt >= TILES_PER_CHUNK
             z_words = z_rows[bt][:].bitcast(F32)
             passes = halves_of(part)
-            turned = turn_banks.tile([P, len(passes), 2, P], F32, tag="turn")
-            if after_passes:
+            pool, tag = (gate_banks, "gate") if second_chunk else (turn_banks, "turn")
+            turned = pool.tile([P, len(passes), 2, P], F32, tag=tag)
+            if second_chunk:
                 bridge(turned[:, 0, 0, 0:BRIDGE_COLS])
             for at, g in enumerate(passes):
                 for u in range(2):
@@ -175,7 +178,8 @@ def tile_lstmcell_pa_kernel(
                     )
             if part is None or part == 0:
                 grouped[bt] = prep.tile([P, K_GROUPS, P, PACK], BF16, align_bytes=64, name="grouped")
-            nc.scalar.copy(
+            copy = nc.vector.tensor_copy if second_chunk and bt % 2 else nc.scalar.copy
+            copy(
                 out=grouped[bt][:, passes[0] : passes[-1] + 1, :, :].bitcast(F32),
                 in_=turned[:].rearrange("p g u b -> p g b u"),
             )
@@ -224,6 +228,7 @@ def tile_lstmcell_pa_kernel(
             for b0, nb, j in group:
                 cells[b0, j] = work.tile([P, nb], F32, name="cell_t")
                 nc.vector.tensor_tensor(out=cells[b0, j][:], in0=acts["i", b0, j][:], in1=acts["g", b0, j][:], op=ALU.mult)
+
             def add_f():
                 for b0, nb, j in group:
                     nc.vector.tensor_tensor(out=cells[b0, j][:], in0=cells[b0, j][:], in1=acts["f", b0, j][:], op=ALU.add)
@@ -317,33 +322,40 @@ def tile_lstmcell_pa_kernel(
 
         steps = [(c * B_CHUNK, B_CHUNK, j) for c in range(CHUNKS) for j in range(N_TILES)]
         steps[-1:] = [(b0, HALF_ROWS, N_TILES - 1) for b0 in (B_CHUNK, B_CHUNK + HALF_ROWS)]
-        first_group = 2
         turned_gates = {}
         turned_back = {}
+
+        def steps_to_turn_back(s):
+            if s < FIRST_GROUP or s > len(steps):
+                return ()
+            return range(FIRST_GROUP) if s == FIRST_GROUP else (s - 1,)
+
+        def z_tiles(s, lag):
+            bt = TILES_PER_CHUNK + s - Z_FIRST_STEP - lag
+            return (bt,) if TILES_PER_CHUNK <= bt < B_TILES else ()
+
         for s in range(len(steps) + 2):
-            prepare = False
-            if s < len(steps):
-                b0, nb, j = steps[s]
-                ahead = TILES_PER_CHUNK + j - Z_PREP_FIRST_STEP
-                prepare = b0 == 0 and TILES_PER_CHUNK <= ahead < B_TILES
-                quantise = b0 == 0 and TILES_PER_CHUNK < ahead <= B_TILES
-                if prepare:
-                    add_z(ahead)
-                if s == 0:
-                    for at, result in enumerate(gates_of(steps[:first_group], False)):
-                        turned_gates[at] = result
-                elif s >= first_group:
-                    turned_gates[s] = gates_of(steps[s : s + 1], s > 1)[0]
-                if quantise:
-                    quantise_z(ahead - 1)
-                if prepare:
-                    turn_z(ahead, after_passes=True)
-            if 0 <= s - 1 < len(steps):
-                turned_back[s - 1] = turn_back(
-                    steps[s - 1], s == len(steps), *turned_gates[s - 1], after_passes=s < len(steps) and not prepare
+            z_to_turn = z_tiles(s, 1)
+            for bt in z_tiles(s, 2):
+                quantise_z(bt)
+            for bt in z_tiles(s, 0):
+                add_z(bt)
+            if s == 0:
+                for at, result in enumerate(gates_of(steps[:FIRST_GROUP], after_transposes=False)):
+                    turned_gates[at] = result
+            elif FIRST_GROUP <= s < len(steps):
+                turned_gates[s] = gates_of(steps[s : s + 1], after_transposes=True)[0]
+            for bt in z_to_turn:
+                turn_z(bt)
+            for at, back in enumerate(steps_to_turn_back(s)):
+                turned_back[back] = turn_back(
+                    steps[back],
+                    back == len(steps) - 1,
+                    *turned_gates[back],
+                    after_passes=s < len(steps) and not z_to_turn and at == 0,
                 )
             for add_f in open_cells:
                 add_f()
             open_cells.clear()
-            if 0 <= s - 2:
-                hidden(steps[s - 2], s - 1 == len(steps), *turned_back[s - 2])
+            if s >= 2:
+                hidden(steps[s - 2], s - 2 == len(steps) - 1, *turned_back[s - 2])

from contextlib import ExitStack

import concourse.mybir as mybir
from concourse.masks import make_identity

F32 = mybir.dt.float32
BF16 = mybir.dt.bfloat16
I32 = mybir.dt.int32
U32 = mybir.dt.uint32
U8 = mybir.dt.uint8
FP8X4 = mybir.dt.float8_e4m3fn_x4
ACT = mybir.ActivationFunctionType
ALU = mybir.AluOpType

P = 128
PACK = 4
K_PASS = P * PACK
B = 1024
H = 1024
K_GROUPS = H // K_PASS
N_TILES = H // P
B_TILES = B // P
B_CHUNK = 512
CHUNKS = B // B_CHUNK
TILES_PER_CHUNK = B_CHUNK // P
PLANE_ROWS = 4
LOAD_COLS = 256
STEPS_PER_STORE = 2
STORE_COLS = STEPS_PER_STORE * P
BRIDGE_COLS = 32
HALF_ROWS = 256
FIRST_GROUP = LOAD_COLS // P
IDLE_MATMULS = (2, 2, 2, 3)
Z_FIRST_STEP = FIRST_GROUP

GATES = ("i", "g", "f", "o")
GATE_FUNC = {"i": ACT.Sigmoid, "g": ACT.Tanh, "f": ACT.Sigmoid, "o": ACT.Sigmoid}

FLOPS = 2 * B * H * 4 * H


def tile_lstmcell_pa_kernel(
    tc,
    inputs,
    short_term_memory,
    Wf_words,
    Wf_scales,
    b_f,
    Wi_words,
    Wi_scales,
    b_i,
    Wg_words,
    Wg_scales,
    b_g,
    Wo_words,
    Wo_scales,
    b_o,
    out,
):
    nc = tc.nc
    words_in = {"i": Wi_words, "g": Wg_words, "f": Wf_words, "o": Wo_words}
    scales_in = {"i": Wi_scales, "g": Wg_scales, "f": Wf_scales, "o": Wo_scales}
    bias_in = {"i": b_i, "g": b_g, "f": b_f, "o": b_o}
    out_view = out.rearrange("o (c t p) n -> o c p t n", t=TILES_PER_CHUNK, p=P)

    with ExitStack() as ctx:
        keep = ctx.enter_context(tc.tile_pool(name="keep", bufs=1))
        rows = ctx.enter_context(tc.tile_pool(name="rows", bufs=B_TILES))
        prep = ctx.enter_context(tc.tile_pool(name="prep", bufs=3))
        work = ctx.enter_context(tc.tile_pool(name="work", bufs=3))
        stage = ctx.enter_context(tc.tile_pool(name="stage", bufs=4))
        gate_banks = ctx.enter_context(tc.psum_pool(name="gate_banks", bufs=4))
        turn_banks = ctx.enter_context(tc.psum_pool(name="turn_banks", bufs=4))
        ctx.enter_context(tc.manual_schedule())

        bias_rows = keep.tile([P, P], BF16)
        nc.gpsimd.memset(bias_rows[:], 0.0)
        for q, gate in enumerate(GATES):
            nc.scalar.dma_start(
                out=bias_rows[N_TILES * q : N_TILES * (q + 1), :],
                in_=bias_in[gate].rearrange("(j n) -> j n", n=P),
            )
        first_in = keep.tile([P, 1], F32)
        nc.gpsimd.memset(first_in[:], 0.0)
        first_out = keep.tile([P, 1], F32)
        nc.scalar.activation(out=first_out[:], in_=first_in[:], func=ACT.Sigmoid)
        ident = keep.tile([P, P], F32)
        make_identity(nc, ident[:])

        w_planes = keep.tile([P, len(GATES), K_GROUPS, H], U8, align_bytes=64)
        nc.vector.memset(w_planes[:].bitcast(I32), 0)

        w_codes = {}
        for gate in GATES:
            w_codes[gate] = keep.tile([P, K_GROUPS, H], U32, align_bytes=64, name="w_codes_" + gate)
        z_codes = []
        z_planes = []
        for c in range(CHUNKS):
            z_codes.append(keep.tile([P, K_GROUPS, B_CHUNK], U32, align_bytes=64, name="z_codes%d" % c))
            z_planes.append(keep.tile([P, K_GROUPS, B_CHUNK], U8, align_bytes=64, name="z_planes%d" % c))

        x_rows = []
        h_rows = []

        def load_rows(bt):
            b_rows = slice(bt * P, (bt + 1) * P)
            x_rows.append(rows.tile([P, H], BF16, name="x_rows"))
            nc.sync.dma_start(out=x_rows[bt][:], in_=inputs[b_rows, :])
            h_rows.append(rows.tile([P, H], BF16, name="h_rows"))
            nc.sync.dma_start(out=h_rows[bt][:], in_=short_term_memory[b_rows, :])

        def load_scales(gate):
            q = GATES.index(gate)
            by_row = scales_in[gate].rearrange("g (Q r) n -> r Q g n", r=PLANE_ROWS)
            for r in range(PLANE_ROWS):
                nc.sync.dma_start(
                    out=w_planes[PLANE_ROWS * q + r : P : 32, q, :, :].bitcast(I32),
                    in_=by_row[r].bitcast(I32),
                )

        def load_words(gate, piece):
            lo, hi = piece * LOAD_COLS, (piece + 1) * LOAD_COLS
            by_partition = words_in[gate].rearrange("g p n t -> p g (n t)")
            nc.sync.dma_start(
                out=w_codes[gate][:, :, lo:hi].bitcast(I32),
                in_=by_partition[:, :, lo * PACK : hi * PACK].bitcast(I32),
            )

        for bt in range(TILES_PER_CHUNK):
            load_rows(bt)
        for gate in GATES:
            load_scales(gate)
            load_words(gate, 0)
        for gate in GATES:
            load_words(gate, 1)
        for bt in range(TILES_PER_CHUNK, B_TILES):
            load_rows(bt)
        for piece in range(2, H // LOAD_COLS):
            for gate in GATES:
                load_words(gate, piece)

        z_rows = {}
        grouped = {}

        def halves_of(part):
            return range(K_GROUPS) if part is None else (part,)

        def add_z(bt, part=None):
            if part is None or part == 0:
                z_rows[bt] = prep.tile([P, H], BF16, name="z_rows")
            in_order = "p (g q u e) -> p g u q e"
            out_order = "p (g u q e) -> p g u q e"
            for g in halves_of(part):
                nc.vector.tensor_tensor(
                    out=z_rows[bt][:].rearrange(out_order, g=K_GROUPS, u=2, e=2)[:, g],
                    in0=x_rows[bt][:].rearrange(in_order, g=K_GROUPS, u=2, e=2)[:, g],
                    in1=h_rows[bt][:].rearrange(in_order, g=K_GROUPS, u=2, e=2)[:, g],
                    op=ALU.add,
                )

        def bridge(bank_cols):
            nc.tensor.matmul(out=bank_cols, lhsT=idle_in[:, 0:P], rhs=idle_in[:, 0:BRIDGE_COLS], start=True, stop=True)

        def turn_z(bt, part=None):
            second_chunk = bt >= TILES_PER_CHUNK
            z_words = z_rows[bt][:].bitcast(F32)
            passes = halves_of(part)
            pool, tag = (gate_banks, "gate") if second_chunk else (turn_banks, "turn")
            turned = pool.tile([P, len(passes), 2, P], F32, tag=tag)
            if second_chunk:
                bridge(turned[:, 0, 0, 0:BRIDGE_COLS])
            for at, g in enumerate(passes):
                for u in range(2):
                    nc.tensor.transpose(
                        turned[:, at, u, :],
                        z_words[:, (K_PASS // 2) * g + P * u : (K_PASS // 2) * g + P * (u + 1)],
                        ident[:],
                    )
            if part is None or part == 0:
                grouped[bt] = prep.tile([P, K_GROUPS, P, PACK], BF16, align_bytes=64, name="grouped")
            copy = nc.vector.tensor_copy if second_chunk and bt % 2 else nc.scalar.copy
            copy(
                out=grouped[bt][:, passes[0] : passes[-1] + 1, :, :].bitcast(F32),
                in_=turned[:].rearrange("p g u b -> p g b u"),
            )

        def quantise_z(bt, part=None):
            c = bt // TILES_PER_CHUNK
            b_cols = slice((bt % TILES_PER_CHUNK) * P, (bt % TILES_PER_CHUNK + 1) * P)
            for g in halves_of(part):
                nc.vector.quantize_mx(
                    out=z_codes[c][:, g, b_cols].bitcast(FP8X4),
                    scales=z_planes[c][:, g, b_cols],
                    in_=grouped[bt][:, g, :, :].rearrange("p b t -> p (b t)"),
                )

        open_cells = []

        def gates_of(group, after_transposes):
            acts = {}
            for q, gate in enumerate(GATES):
                for b0, nb, j in group:
                    n_cols = slice(j * P, (j + 1) * P)
                    c = b0 // B_CHUNK
                    b_cols = slice(b0 % B_CHUNK, b0 % B_CHUNK + nb)
                    bank = gate_banks.tile([P, B_CHUNK], F32, tag="gate")
                    if after_transposes and q == 0:
                        bridge(bank[:, 0:BRIDGE_COLS])
                    for g in range(K_GROUPS):
                        nc.tensor.matmul_mx(
                            out=bank[:, 0:nb],
                            lhsT=w_codes[gate][:, g, n_cols].bitcast(FP8X4),
                            lhsT_scale=w_planes[PLANE_ROWS * q : P, q, g, n_cols],
                            rhs=z_codes[c][:, g, b_cols].bitcast(FP8X4),
                            rhs_scale=z_planes[c][:, g, b_cols],
                            start=(g == 0),
                            stop=(g == K_GROUPS - 1),
                        )
                    acts[gate, b0, j] = work.tile([P, nb], F32, name="act_" + gate)
                    nc.scalar.activation(
                        out=acts[gate, b0, j][:],
                        in_=bank[:, 0:nb],
                        func=GATE_FUNC[gate],
                        bias=bias_cols[:, N_TILES * q + j : N_TILES * q + j + 1],
                        scale=1.0,
                    )
            cells = {}
            for b0, nb, j in group:
                cells[b0, j] = work.tile([P, nb], F32, name="cell_t")
                nc.vector.tensor_tensor(out=cells[b0, j][:], in0=acts["i", b0, j][:], in1=acts["g", b0, j][:], op=ALU.mult)

            def add_f():
                for b0, nb, j in group:
                    nc.vector.tensor_tensor(out=cells[b0, j][:], in0=cells[b0, j][:], in1=acts["f", b0, j][:], op=ALU.add)

            if len(group) > 1:
                add_f()
            else:
                open_cells.append(add_f)
            return [(cells[b0, j], acts["o", b0, j]) for b0, nb, j in group]

        staged = {}

        def stage_cols(j):
            return slice((j % STEPS_PER_STORE) * P, (j % STEPS_PER_STORE + 1) * P)

        def stage_for(which, step):
            b0, nb, j = step
            if j % STEPS_PER_STORE == 0 or nb < B_CHUNK:
                staged[which] = stage.tile([P, nb // P, STORE_COLS], F32, name=which + "_stage")

        def store(which, o, step):
            b0, nb, j = step
            c = b0 // B_CHUNK
            tiles = slice(b0 % B_CHUNK // P, (b0 % B_CHUNK + nb) // P)
            if c == CHUNKS - 1 and j >= N_TILES - STEPS_PER_STORE:
                nc.sync.dma_start(out=out_view[o, c, :, tiles, j * P : (j + 1) * P], in_=staged[which][:, :, stage_cols(j)])
            elif j % STEPS_PER_STORE == STEPS_PER_STORE - 1:
                n_cols = slice((j + 1) * P - STORE_COLS, (j + 1) * P)
                nc.sync.dma_start(out=out_view[o, c, :, tiles, n_cols], in_=staged[which][:])

        def turn_back(step, last, cell_t, gate_o_t, after_passes):
            b0, nb, j = step
            stage_for("c", step)
            if nb == B_CHUNK:
                whole_c = turn_banks.tile([P, nb // P, P], F32, tag="turn")
                whole_o = turn_banks.tile([P, nb // P, P], F32, tag="turn")
                c_bank, o_bank = whole_c[:], whole_o[:]
            else:
                both = turn_banks.tile([P, 2, nb // P, P], F32, tag="turn", name="both")
                c_bank, o_bank = both[:, 0], both[:, 1]
            if after_passes:
                bridge(c_bank[:, 0, 0:BRIDGE_COLS])
            for t in range(nb // P):
                nc.tensor.transpose(c_bank[:, t, :], cell_t[:, t * P : (t + 1) * P], ident[:])
            for t in range(nb // P):
                nc.tensor.transpose(o_bank[:, t, :], gate_o_t[:, t * P : (t + 1) * P], ident[:])
            if last:
                return c_bank, o_bank
            c_cols = staged["c"][:, :, stage_cols(j)]
            nc.vector.tensor_copy(out=c_cols, in_=c_bank)
            store("c", 0, step)
            return c_cols, o_bank

        def hidden(step, last, c_cols, o_bank):
            b0, nb, j = step
            stage_for("h", step)
            tanh_c = work.tile([P, nb // P, P], F32, name="tanh_c")
            nc.scalar.activation(out=tanh_c[:], in_=c_cols, func=ACT.Tanh)
            if last:
                nc.scalar.copy(out=staged["c"][:, :, stage_cols(j)], in_=c_cols)
                store("c", 0, step)
            nc.vector.tensor_tensor(out=staged["h"][:, :, stage_cols(j)], in0=o_bank, in1=tanh_c[:], op=ALU.mult)
            store("h", 1, step)

        last_tile = TILES_PER_CHUNK - 1
        idle_in = keep.tile([P, B_CHUNK], BF16)
        nc.gpsimd.memset(idle_in[:], 0.0)
        idle_bank = gate_banks.tile([P, B_CHUNK], F32, tag="gate", name="idle_bank")
        bias_f32 = keep.tile([P, P], F32)
        bias_cols = keep.tile([P, P], F32)
        for bt in range(last_tile):
            add_z(bt)
            turn_z(bt)
            for rep in range(IDLE_MATMULS[bt]):
                nc.tensor.matmul(out=idle_bank[:], lhsT=idle_in[:, 0:P], rhs=idle_in[:], start=True, stop=True)
            if bt == 1:
                quantise_z(0)
        for g in range(K_GROUPS):
            add_z(last_tile, g)
            turn_z(last_tile, g)
        nc.vector.tensor_copy(out=bias_f32[:], in_=bias_rows[:])
        bias_bank = turn_banks.tile([P, P], F32, tag="turn", name="bias_bank")
        nc.tensor.transpose(bias_bank[:], bias_f32[:], ident[:])
        for rep in range(IDLE_MATMULS[last_tile]):
            nc.tensor.matmul(out=idle_bank[:], lhsT=idle_in[:, 0:P], rhs=idle_in[:], start=True, stop=True)
        quantise_z(1)
        quantise_z(2)
        nc.vector.tensor_copy(out=bias_cols[:], in_=bias_bank[:])
        for g in range(K_GROUPS):
            quantise_z(last_tile, g)

        steps = [(c * B_CHUNK, B_CHUNK, j) for c in range(CHUNKS) for j in range(N_TILES)]
        steps[-1:] = [(b0, HALF_ROWS, N_TILES - 1) for b0 in (B_CHUNK, B_CHUNK + HALF_ROWS)]
        turned_gates = {}
        turned_back = {}

        def steps_to_turn_back(s):
            if s < FIRST_GROUP or s > len(steps):
                return ()
            return range(FIRST_GROUP) if s == FIRST_GROUP else (s - 1,)

        def z_tiles(s, lag):
            bt = TILES_PER_CHUNK + s - Z_FIRST_STEP - lag
            return (bt,) if TILES_PER_CHUNK <= bt < B_TILES else ()

        for s in range(len(steps) + 2):
            z_to_turn = z_tiles(s, 1)
            for bt in z_tiles(s, 2):
                quantise_z(bt)
            for bt in z_tiles(s, 0):
                add_z(bt)
            if s == 0:
                for at, result in enumerate(gates_of(steps[:FIRST_GROUP], after_transposes=False)):
                    turned_gates[at] = result
            elif FIRST_GROUP <= s < len(steps):
                turned_gates[s] = gates_of(steps[s : s + 1], after_transposes=True)[0]
            for bt in z_to_turn:
                turn_z(bt)
            for at, back in enumerate(steps_to_turn_back(s)):
                turned_back[back] = turn_back(
                    steps[back],
                    back == len(steps) - 1,
                    *turned_gates[back],
                    after_passes=s < len(steps) and not z_to_turn and at == 0,
                )
            for add_f in open_cells:
                add_f()
            open_cells.clear()
            if s >= 2:
                hidden(steps[s - 2], s - 2 == len(steps) - 1, *turned_back[s - 2])
